import numpy as np
import ml_dtypes


def mxq(x, axis, fmt="e4m3"):
    dtype, down = {"e4m3": (ml_dtypes.float8_e4m3fn, 7), "e5m2": (ml_dtypes.float8_e5m2, 14)}[fmt]
    v = np.moveaxis(np.asarray(x, np.float32).astype(ml_dtypes.bfloat16).astype(np.float64), axis, -1)
    blocks = v.reshape(v.shape[:-1] + (-1, 32))
    amax = np.abs(blocks).max(-1, keepdims=True)
    byte = np.maximum(np.where(amax > 0, np.frexp(amax)[1] - 1 + 127, 0) - down, 1)
    scale = np.exp2(byte - 127.0)
    codes = (blocks / scale).astype(np.float32).astype(dtype).astype(np.float64)
    return np.moveaxis((codes * scale).reshape(v.shape), -1, axis)


WIDE = False


def mx_kscale(k):
    if not WIDE:
        return np.ones(k)
    levels = np.array([10, -10, 5, -5, 0])
    a = np.random.permutation(np.resize(levels, k // 512 * 4)).reshape(k // 512, 4)
    idx = np.arange(k)
    return np.exp2(a[idx // 512, idx % 128 // 32])


BF16 = ml_dtypes.bfloat16


def bf(x):
    return np.asarray(x, np.float32).astype(BF16)


def f64(x):
    return np.asarray(x).astype(np.float64)


N, E, D = 1024, 1024, 128


def setup_inputs():
    s = mx_kscale(N)
    s = s / np.exp2(np.round(np.log2(s.mean())))
    return {"X": bf(np.random.standard_normal((N, D)) * 0.5 * np.sqrt(N) / s[:, None]),
            "H": bf(np.random.uniform(0.0, 1.0, (N, E)) * (16.0 / N) * s[:, None])}


def reference(X, H):
    Hf = f64(H)
    msg = mxq(Hf, 0, "e4m3").T @ mxq(f64(X), 0, "e4m3")
    with np.errstate(divide="ignore"):
        inv_deg = 1.0 / Hf.sum(axis=0)
    inv_deg = np.where(np.isinf(inv_deg), 0.0, inv_deg)
    return msg * inv_deg[:, None]

@@ -1,0 +1,173 @@
+from contextlib import ExitStack
+
+import concourse.mybir as mybir
+
+BF16 = mybir.dt.bfloat16
+F32 = mybir.dt.float32
+U32 = mybir.dt.uint32
+U8 = mybir.dt.uint8
+FP8X4 = mybir.dt.float8_e4m3fn_x4
+ALU = mybir.AluOpType
+ACT = mybir.ActivationFunctionType
+AXIS = mybir.AxisListType
+
+P = 128
+PACK = 4
+K_PASS = P * PACK
+VERTICES = 1024
+EDGES = 1024
+FEATURES = 128
+PASSES = VERTICES // K_PASS
+E_TILE = 128
+CHUNK = 512
+TILES = CHUNK // E_TILE
+CHUNKS = EDGES // CHUNK
+RUN = 4
+PSUM_BANKS = 8
+
+FLOPS = 2 * VERTICES * EDGES * FEATURES
+
+
+def regroup(copy, grouped, rows):
+    copy(
+        out=grouped.rearrange("p (g i) j -> p g j i", i=RUN),
+        in_=rows.rearrange("p j (g i) -> p g j i", i=RUN),
+    )
+
+
+def tile_v2emsgpass_s_kernel(tc, X, H, out):
+    nc = tc.nc
+    with ExitStack() as ctx:
+        consts = ctx.enter_context(tc.tile_pool(name="consts", bufs=1))
+        raw_pool = ctx.enter_context(tc.tile_pool(name="raw", bufs=CHUNKS * PASSES))
+        mx_pool = ctx.enter_context(tc.tile_pool(name="mx", bufs=CHUNKS * PASSES * TILES))
+        deg_pool = ctx.enter_context(tc.tile_pool(name="deg", bufs=CHUNKS))
+        res_pool = ctx.enter_context(tc.tile_pool(name="res", bufs=CHUNKS * TILES))
+        deg_psum = ctx.enter_context(tc.psum_pool(name="deg_psum", bufs=CHUNKS))
+        acc_psum = ctx.enter_context(tc.psum_pool(name="acc_psum", bufs=PSUM_BANKS - CHUNKS))
+        ctx.enter_context(tc.manual_schedule())
+
+        x_raw = consts.tile([P, PASSES, PACK, FEATURES], BF16)
+        nc.sync.dma_start(out=x_raw[:], in_=X.rearrange("(c p j) d -> p c j d", c=PASSES, j=PACK))
+        h_raw = {}
+        for h in range(CHUNKS):
+            for c in range(PASSES):
+                raw = raw_pool.tile([P, PACK, CHUNK], BF16)
+                nc.sync.dma_start(
+                    out=raw[:],
+                    in_=H[c * K_PASS : (c + 1) * K_PASS, h * CHUNK : (h + 1) * CHUNK].rearrange(
+                        "(p j) e -> p j e", j=PACK
+                    ),
+                )
+                h_raw[(h, c)] = raw
+
+        ones = consts.tile([P, 1], BF16)
+        nc.vector.memset(ones[:], 1.0)
+        table_warm = consts.tile([P, 1], F32)
+        nc.scalar.activation(out=table_warm[:], in_=ones[:], func=ACT.Copy)
+
+        x_grouped = consts.tile([P, PASSES, FEATURES, PACK], BF16, align_bytes=64)
+        x_codes = consts.tile([P, PASSES, FEATURES], U32, align_bytes=64)
+        x_scales = consts.tile([P, PASSES, FEATURES], U8, align_bytes=64)
+        for c in range(PASSES):
+            regroup(nc.vector.tensor_copy, x_grouped[:, c], x_raw[:, c])
+        nc.vector.quantize_mx(
+            out=x_codes[:].rearrange("p c d -> p (c d)").bitcast(FP8X4),
+            scales=x_scales[:].rearrange("p c d -> p (c d)"),
+            in_=x_grouped[:].rearrange("p c d j -> p (c d j)"),
+        )
+
+        def scale_and_store(h, acc, inv_deg):
+            for t in range(TILES):
+                res = res_pool.tile([P, FEATURES], F32)
+                if t % 2 == 0:
+                    nc.scalar.activation(
+                        out=res[:], in_=acc[t][:], func=ACT.Copy, scale=inv_deg[:, t : t + 1]
+                    )
+                else:
+                    nc.vector.tensor_scalar(
+                        out=res[:],
+                        in0=acc[t][:],
+                        scalar1=inv_deg[:, t : t + 1],
+                        scalar2=None,
+                        op0=ALU.mult,
+                    )
+                first_row = h * CHUNK + t * E_TILE
+                nc.sync.dma_start(out=out[first_row : first_row + E_TILE, :], in_=res[:])
+
+        finished = None
+        for h in range(CHUNKS):
+            deg_ps = deg_psum.tile([P, PASSES, TILES], F32)
+            deg = deg_pool.tile([P, TILES], F32)
+            safe_deg = deg_pool.tile([P, TILES], F32)
+            recip = deg_pool.tile([P, TILES], F32)
+            inv_deg = deg_pool.tile([P, TILES], F32)
+            acc = []
+
+            for c in range(PASSES):
+                raw = h_raw[(h, c)]
+                last_pass = c == PASSES - 1
+
+                grouped = []
+                for t in range(TILES):
+                    grouped_t = mx_pool.tile([P, E_TILE, PACK], BF16, align_bytes=64)
+                    grouped.append(grouped_t)
+                    copy = nc.vector.tensor_copy if t % 2 == 0 else nc.scalar.copy
+                    regroup(copy, grouped_t[:], raw[:, :, t * E_TILE : (t + 1) * E_TILE])
+
+                if finished is not None:
+                    scale_and_store(*finished)
+                    finished = None
+
+                for t in range(TILES):
+                    for j in range(PACK):
+                        nc.tensor.matmul(
+                            out=deg_ps[:, c, t : t + 1],
+                            lhsT=raw[:, j, t * E_TILE : (t + 1) * E_TILE],
+                            rhs=ones[:],
+                            start=(j == 0),
+                            stop=(j == PACK - 1),
+                        )
+
+                codes = []
+                scales = []
+                for t in range(TILES):
+                    codes_t = mx_pool.tile([P, E_TILE], U32, align_bytes=64)
+                    scales_t = mx_pool.tile([P, E_TILE], U8, align_bytes=64)
+                    codes.append(codes_t)
+                    scales.append(scales_t)
+                    nc.vector.quantize_mx(
+                        out=codes_t[:].bitcast(FP8X4),
+                        scales=scales_t[:],
+                        in_=grouped[t][:].rearrange("p w j -> p (w j)"),
+                    )
+                    if last_pass and t == 0:
+                        nc.vector.tensor_reduce(
+                            out=deg[:], in_=deg_ps[:].rearrange("p c t -> p t c"), axis=AXIS.X, op=ALU.add
+                        )
+                    if last_pass and t == 1:
+                        nc.vector.scalar_tensor_tensor(
+                            out=safe_deg[:], in0=deg[:], scalar=0.0, in1=deg[:], op0=ALU.is_equal, op1=ALU.add
+                        )
+                    if last_pass and t == 2:
+                        nc.vector.reciprocal(out=recip[:], in_=safe_deg[:])
+                    if last_pass and t == 3:
+                        nc.vector.scalar_tensor_tensor(
+                            out=inv_deg[:], in0=deg[:], scalar=0.0, in1=recip[:], op0=ALU.not_equal, op1=ALU.mult
+                        )
+
+                for t in range(TILES):
+                    if c == 0:
+                        acc_t = acc_psum.tile([P, FEATURES], F32)
+                        acc.append(acc_t)
+                    nc.tensor.matmul_mx(
+                        out=acc[t][:],
+                        lhsT=codes[t][:].bitcast(FP8X4),
+                        lhsT_scale=scales[t][:],
+                        rhs=x_codes[:, c, :].bitcast(FP8X4),
+                        rhs_scale=x_scales[:, c, :],
+                        start=(c == 0),
+                        stop=last_pass,
+                    )
+            finished = (h, acc, inv_deg)
+        scale_and_store(*finished)

@@ -24,6 +24,7 @@ TILES = CHUNK // E_TILE
 CHUNKS = EDGES // CHUNK
 RUN = 4
 PSUM_BANKS = 8
+TILE_ORDER = list(range(0, TILES, 2)) + list(range(1, TILES, 2))
 
 FLOPS = 2 * VERTICES * EDGES * FEATURES
 
@@ -77,10 +78,10 @@ def tile_v2emsgpass_s_kernel(tc, X, H, out):
             in_=x_grouped[:].rearrange("p c d j -> p (c d j)"),
         )
 
-        def scale_and_store(h, acc, inv_deg):
-            for t in range(TILES):
+        def scale_and_store(h, acc, inv_deg, vector_helps):
+            for i, t in enumerate(TILE_ORDER):
                 res = res_pool.tile([P, FEATURES], F32)
-                if t % 2 == 0:
+                if i % 2 == 0 or not vector_helps:
                     nc.scalar.activation(
                         out=res[:], in_=acc[t][:], func=ACT.Copy, scale=inv_deg[:, t : t + 1]
                     )
@@ -102,7 +103,24 @@ def tile_v2emsgpass_s_kernel(tc, X, H, out):
             safe_deg = deg_pool.tile([P, TILES], F32)
             recip = deg_pool.tile([P, TILES], F32)
             inv_deg = deg_pool.tile([P, TILES], F32)
-            acc = []
+            acc = {}
+            codes = {}
+            scales = {}
+
+            def multiply(c):
+                for t in TILE_ORDER:
+                    if c == 0:
+                        acc_t = acc_psum.tile([P, FEATURES], F32)
+                        acc[t] = acc_t
+                    nc.tensor.matmul_mx(
+                        out=acc[t][:],
+                        lhsT=codes[(c, t)][:].bitcast(FP8X4),
+                        lhsT_scale=scales[(c, t)][:],
+                        rhs=x_codes[:, c, :].bitcast(FP8X4),
+                        rhs_scale=x_scales[:, c, :],
+                        start=(c == 0),
+                        stop=(c == PASSES - 1),
+                    )
 
             for c in range(PASSES):
                 raw = h_raw[(h, c)]
@@ -116,7 +134,7 @@ def tile_v2emsgpass_s_kernel(tc, X, H, out):
                     regroup(copy, grouped_t[:], raw[:, :, t * E_TILE : (t + 1) * E_TILE])
 
                 if finished is not None:
-                    scale_and_store(*finished)
+                    scale_and_store(*finished, vector_helps=False)
                     finished = None
 
                 for t in range(TILES):
@@ -129,45 +147,36 @@ def tile_v2emsgpass_s_kernel(tc, X, H, out):
                             stop=(j == PACK - 1),
                         )
 
-                codes = []
-                scales = []
-                for t in range(TILES):
+                if last_pass:
+                    for earlier in range(c):
+                        multiply(earlier)
+
+                for i, t in enumerate(TILE_ORDER):
                     codes_t = mx_pool.tile([P, E_TILE], U32, align_bytes=64)
                     scales_t = mx_pool.tile([P, E_TILE], U8, align_bytes=64)
-                    codes.append(codes_t)
-                    scales.append(scales_t)
+                    codes[(c, t)] = codes_t
+                    scales[(c, t)] = scales_t
                     nc.vector.quantize_mx(
                         out=codes_t[:].bitcast(FP8X4),
                         scales=scales_t[:],
                         in_=grouped[t][:].rearrange("p w j -> p (w j)"),
                     )
-                    if last_pass and t == 0:
+                    if last_pass and i == 0:
                         nc.vector.tensor_reduce(
                             out=deg[:], in_=deg_ps[:].rearrange("p c t -> p t c"), axis=AXIS.X, op=ALU.add
                         )
-                    if last_pass and t == 1:
+                    if last_pass and i == 1:
                         nc.vector.scalar_tensor_tensor(
                             out=safe_deg[:], in0=deg[:], scalar=0.0, in1=deg[:], op0=ALU.is_equal, op1=ALU.add
                         )
-                    if last_pass and t == 2:
+                    if last_pass and i == 2:
                         nc.vector.reciprocal(out=recip[:], in_=safe_deg[:])
-                    if last_pass and t == 3:
+                    if last_pass and i == 3:
                         nc.vector.scalar_tensor_tensor(
                             out=inv_deg[:], in0=deg[:], scalar=0.0, in1=recip[:], op0=ALU.not_equal, op1=ALU.mult
                         )
 
-                for t in range(TILES):
-                    if c == 0:
-                        acc_t = acc_psum.tile([P, FEATURES], F32)
-                        acc.append(acc_t)
-                    nc.tensor.matmul_mx(
-                        out=acc[t][:],
-                        lhsT=codes[t][:].bitcast(FP8X4),
-                        lhsT_scale=scales[t][:],
-                        rhs=x_codes[:, c, :].bitcast(FP8X4),
-                        rhs_scale=x_scales[:, c, :],
-                        start=(c == 0),
-                        stop=last_pass,
-                    )
+                if last_pass:
+                    multiply(c)
             finished = (h, acc, inv_deg)
-        scale_and_store(*finished)
+        scale_and_store(*finished, vector_helps=True)

@@ -18,13 +18,14 @@ VERTICES = 1024
 EDGES = 1024
 FEATURES = 128
 PASSES = VERTICES // K_PASS
+LAST = PASSES - 1
 E_TILE = 128
-CHUNK = 512
-TILES = CHUNK // E_TILE
-CHUNKS = EDGES // CHUNK
 RUN = 4
 PSUM_BANKS = 8
-TILE_ORDER = list(range(0, TILES, 2)) + list(range(1, TILES, 2))
+DEG_BANKS = 2
+GROUP_TILES = (2, 4, 2)
+VECTOR_SHARE = (8, 16)
+X_BEHIND = 0
 
 FLOPS = 2 * VERTICES * EDGES * FEATURES
 
@@ -39,144 +40,180 @@ def regroup(copy, grouped, rows):
 def tile_v2emsgpass_s_kernel(tc, X, H, out):
     nc = tc.nc
     with ExitStack() as ctx:
-        consts = ctx.enter_context(tc.tile_pool(name="consts", bufs=1))
-        raw_pool = ctx.enter_context(tc.tile_pool(name="raw", bufs=CHUNKS * PASSES))
-        mx_pool = ctx.enter_context(tc.tile_pool(name="mx", bufs=CHUNKS * PASSES * TILES))
-        deg_pool = ctx.enter_context(tc.tile_pool(name="deg", bufs=CHUNKS))
-        res_pool = ctx.enter_context(tc.tile_pool(name="res", bufs=CHUNKS * TILES))
-        deg_psum = ctx.enter_context(tc.psum_pool(name="deg_psum", bufs=CHUNKS))
-        acc_psum = ctx.enter_context(tc.psum_pool(name="acc_psum", bufs=PSUM_BANKS - CHUNKS))
+        keep = ctx.enter_context(tc.tile_pool(name="keep", bufs=1))
+        deg_psum = ctx.enter_context(tc.psum_pool(name="deg_psum", bufs=DEG_BANKS))
+        acc_psum = ctx.enter_context(tc.psum_pool(name="acc_psum", bufs=PSUM_BANKS - DEG_BANKS))
         ctx.enter_context(tc.manual_schedule())
 
-        x_raw = consts.tile([P, PASSES, PACK, FEATURES], BF16)
-        nc.sync.dma_start(out=x_raw[:], in_=X.rearrange("(c p j) d -> p c j d", c=PASSES, j=PACK))
-        h_raw = {}
-        for h in range(CHUNKS):
-            for c in range(PASSES):
-                raw = raw_pool.tile([P, PACK, CHUNK], BF16)
-                nc.sync.dma_start(
-                    out=raw[:],
-                    in_=H[c * K_PASS : (c + 1) * K_PASS, h * CHUNK : (h + 1) * CHUNK].rearrange(
-                        "(p j) e -> p j e", j=PACK
-                    ),
-                )
-                h_raw[(h, c)] = raw
+        chunks = [(g, c) for g in range(len(GROUP_TILES)) for c in range(PASSES)]
+        first_tile = [sum(GROUP_TILES[:g]) for g in range(len(GROUP_TILES))]
+        tiles_in_all = sum(GROUP_TILES)
 
-        ones = consts.tile([P, 1], BF16)
+        x_raw = keep.tile([P, PASSES, PACK, FEATURES], BF16, name="x_raw")
+        raw = {}
+        for k, (g, c) in enumerate(chunks):
+            if k == X_BEHIND:
+                nc.sync.dma_start(out=x_raw[:], in_=X.rearrange("(c p j) d -> p c j d", c=PASSES, j=PACK))
+            width = GROUP_TILES[g] * E_TILE
+            raw[(g, c)] = keep.tile([P, PACK, width], BF16, name="raw_%d_%d" % (g, c))
+            nc.sync.dma_start(
+                out=raw[(g, c)][:],
+                in_=H[
+                    c * K_PASS : (c + 1) * K_PASS, first_tile[g] * E_TILE : first_tile[g] * E_TILE + width
+                ].rearrange("(p j) e -> p j e", j=PACK),
+            )
+
+        ones = keep.tile([P, 1], BF16, name="ones")
         nc.vector.memset(ones[:], 1.0)
-        table_warm = consts.tile([P, 1], F32)
+        table_warm = keep.tile([P, 1], F32, name="table_warm")
         nc.scalar.activation(out=table_warm[:], in_=ones[:], func=ACT.Copy)
 
-        x_grouped = consts.tile([P, PASSES, FEATURES, PACK], BF16, align_bytes=64)
-        x_codes = consts.tile([P, PASSES, FEATURES], U32, align_bytes=64)
-        x_scales = consts.tile([P, PASSES, FEATURES], U8, align_bytes=64)
-        for c in range(PASSES):
-            regroup(nc.vector.tensor_copy, x_grouped[:, c], x_raw[:, c])
-        nc.vector.quantize_mx(
-            out=x_codes[:].rearrange("p c d -> p (c d)").bitcast(FP8X4),
-            scales=x_scales[:].rearrange("p c d -> p (c d)"),
-            in_=x_grouped[:].rearrange("p c d j -> p (c d j)"),
-        )
+        x_grouped = keep.tile([P, PASSES, FEATURES, PACK], BF16, name="x_grouped", align_bytes=64)
+        x_codes = keep.tile([P, PASSES, FEATURES], U32, name="x_codes", align_bytes=64)
+        x_scales = keep.tile([P, PASSES, FEATURES], U8, name="x_scales", align_bytes=64)
 
-        def scale_and_store(h, acc, inv_deg, vector_helps):
-            for i, t in enumerate(TILE_ORDER):
-                res = res_pool.tile([P, FEATURES], F32)
-                if i % 2 == 0 or not vector_helps:
-                    nc.scalar.activation(
-                        out=res[:], in_=acc[t][:], func=ACT.Copy, scale=inv_deg[:, t : t + 1]
+        deg_ps = {}
+        deg = keep.tile([P, tiles_in_all], F32, name="deg")
+        safe_deg = keep.tile([P, tiles_in_all], F32, name="safe_deg")
+        recip = keep.tile([P, tiles_in_all], F32, name="recip")
+        inv_deg = keep.tile([P, tiles_in_all], F32, name="inv_deg")
+
+        grouped = {}
+        codes = {}
+        scales = {}
+        acc = {}
+        chains = []
+        scaled = set()
+        quantised = []
+        multiplied = []
+        x_ready = []
+
+        def degree_sums(g, c):
+            if c == 0:
+                deg_ps[g] = deg_psum.tile([P, PASSES, GROUP_TILES[g]], F32, name="deg_ps")
+            for i in range(GROUP_TILES[g]):
+                for j in range(PACK):
+                    nc.tensor.matmul(
+                        out=deg_ps[g][:, c, i : i + 1],
+                        lhsT=raw[(g, c)][:, j, i * E_TILE : (i + 1) * E_TILE],
+                        rhs=ones[:],
+                        start=(j == 0),
+                        stop=(j == PACK - 1),
                     )
-                else:
-                    nc.vector.tensor_scalar(
-                        out=res[:],
-                        in0=acc[t][:],
-                        scalar1=inv_deg[:, t : t + 1],
-                        scalar2=None,
-                        op0=ALU.mult,
-                    )
-                first_row = h * CHUNK + t * E_TILE
-                nc.sync.dma_start(out=out[first_row : first_row + E_TILE, :], in_=res[:])
 
-        finished = None
-        for h in range(CHUNKS):
-            deg_ps = deg_psum.tile([P, PASSES, TILES], F32)
-            deg = deg_pool.tile([P, TILES], F32)
-            safe_deg = deg_pool.tile([P, TILES], F32)
-            recip = deg_pool.tile([P, TILES], F32)
-            inv_deg = deg_pool.tile([P, TILES], F32)
-            acc = {}
-            codes = {}
-            scales = {}
+        def reciprocal_steps(g, cols):
+            return [
+                lambda: nc.vector.tensor_reduce(
+                    out=deg[:, cols], in_=deg_ps[g][:].rearrange("p c t -> p t c"), axis=AXIS.X, op=ALU.add
+                ),
+                lambda: nc.vector.scalar_tensor_tensor(
+                    out=safe_deg[:, cols], in0=deg[:, cols], scalar=0.0, in1=deg[:, cols],
+                    op0=ALU.is_equal, op1=ALU.add,
+                ),
+                lambda: nc.vector.reciprocal(out=recip[:, cols], in_=safe_deg[:, cols]),
+                lambda: nc.vector.scalar_tensor_tensor(
+                    out=inv_deg[:, cols], in0=deg[:, cols], scalar=0.0, in1=recip[:, cols],
+                    op0=ALU.not_equal, op1=ALU.mult,
+                ),
+            ]
 
-            def multiply(c):
-                for t in TILE_ORDER:
+        def start_chain(g):
+            tiles = list(range(first_tile[g], first_tile[g] + GROUP_TILES[g]))
+            chains.append([reciprocal_steps(g, slice(tiles[0], tiles[-1] + 1)), tiles, 0])
+
+        def short_steps():
+            for chain in chains:
+                steps, tiles, done = chain
+                if done < len(steps):
+                    steps[done]()
+                    chain[2] = done + 1
+                    if chain[2] == len(steps):
+                        for t in tiles:
+                            scaled.add(t)
+
+        def multiply():
+            if not x_ready:
+                return
+            for g, c in quantised:
+                for i in range(GROUP_TILES[g]):
                     if c == 0:
-                        acc_t = acc_psum.tile([P, FEATURES], F32)
-                        acc[t] = acc_t
+                        acc_t = acc_psum.tile([P, FEATURES], F32, name="acc")
+                        acc[first_tile[g] + i] = acc_t
                     nc.tensor.matmul_mx(
-                        out=acc[t][:],
-                        lhsT=codes[(c, t)][:].bitcast(FP8X4),
-                        lhsT_scale=scales[(c, t)][:],
+                        out=acc[first_tile[g] + i][:],
+                        lhsT=codes[(g, c)][:, i * E_TILE : (i + 1) * E_TILE].bitcast(FP8X4),
+                        lhsT_scale=scales[(g, c)][:, i * E_TILE : (i + 1) * E_TILE],
                         rhs=x_codes[:, c, :].bitcast(FP8X4),
                         rhs_scale=x_scales[:, c, :],
                         start=(c == 0),
-                        stop=(c == PASSES - 1),
+                        stop=(c == LAST),
                     )
+                    if c == LAST:
+                        multiplied.append(first_tile[g] + i)
+            quantised.clear()
 
-            for c in range(PASSES):
-                raw = h_raw[(h, c)]
-                last_pass = c == PASSES - 1
+        def quantize(g, c):
+            nc.vector.quantize_mx(
+                out=codes[(g, c)][:].bitcast(FP8X4),
+                scales=scales[(g, c)][:],
+                in_=grouped[(g, c)][:].rearrange("p w j -> p (w j)"),
+            )
+            quantised.append((g, c))
+            multiply()
+            short_steps()
 
-                grouped = []
-                for t in range(TILES):
-                    grouped_t = mx_pool.tile([P, E_TILE, PACK], BF16, align_bytes=64)
-                    grouped.append(grouped_t)
-                    copy = nc.vector.tensor_copy if t % 2 == 0 else nc.scalar.copy
-                    regroup(copy, grouped_t[:], raw[:, :, t * E_TILE : (t + 1) * E_TILE])
+        def scale_and_store(t, on_vector):
+            res = keep.tile([P, FEATURES], F32, name="res_%d" % t)
+            if on_vector:
+                nc.vector.tensor_scalar(
+                    out=res[:], in0=acc[t][:], scalar1=inv_deg[:, t : t + 1], scalar2=None, op0=ALU.mult
+                )
+            else:
+                nc.scalar.activation(out=res[:], in_=acc[t][:], func=ACT.Copy, scale=inv_deg[:, t : t + 1])
+            nc.sync.dma_start(out=out[t * E_TILE : (t + 1) * E_TILE, :], in_=res[:])
 
-                if finished is not None:
-                    scale_and_store(*finished, vector_helps=False)
-                    finished = None
+        def regroup_x():
+            for cx in range(PASSES):
+                regroup(nc.vector.tensor_copy, x_grouped[:, cx], x_raw[:, cx])
+                short_steps()
 
-                for t in range(TILES):
-                    for j in range(PACK):
-                        nc.tensor.matmul(
-                            out=deg_ps[:, c, t : t + 1],
-                            lhsT=raw[:, j, t * E_TILE : (t + 1) * E_TILE],
-                            rhs=ones[:],
-                            start=(j == 0),
-                            stop=(j == PACK - 1),
-                        )
+        if X_BEHIND == 0:
+            regroup_x()
+        degree_sums(*chunks[0])
+        for k, (g, c) in enumerate(chunks):
+            width = GROUP_TILES[g] * E_TILE
+            split = width * VECTOR_SHARE[0] // VECTOR_SHARE[1]
+            grouped[(g, c)] = keep.tile([P, width, PACK], BF16, name="grouped_%d_%d" % (g, c), align_bytes=64)
+            codes[(g, c)] = keep.tile([P, width], U32, name="codes_%d_%d" % (g, c), align_bytes=64)
+            scales[(g, c)] = keep.tile([P, width], U8, name="scales_%d_%d" % (g, c), align_bytes=64)
 
-                if last_pass:
-                    for earlier in range(c):
-                        multiply(earlier)
-
-                for i, t in enumerate(TILE_ORDER):
-                    codes_t = mx_pool.tile([P, E_TILE], U32, align_bytes=64)
-                    scales_t = mx_pool.tile([P, E_TILE], U8, align_bytes=64)
-                    codes[(c, t)] = codes_t
-                    scales[(c, t)] = scales_t
-                    nc.vector.quantize_mx(
-                        out=codes_t[:].bitcast(FP8X4),
-                        scales=scales_t[:],
-                        in_=grouped[t][:].rearrange("p w j -> p (w j)"),
-                    )
-                    if last_pass and i == 0:
-                        nc.vector.tensor_reduce(
-                            out=deg[:], in_=deg_ps[:].rearrange("p c t -> p t c"), axis=AXIS.X, op=ALU.add
-                        )
-                    if last_pass and i == 1:
-                        nc.vector.scalar_tensor_tensor(
-                            out=safe_deg[:], in0=deg[:], scalar=0.0, in1=deg[:], op0=ALU.is_equal, op1=ALU.add
-                        )
-                    if last_pass and i == 2:
-                        nc.vector.reciprocal(out=recip[:], in_=safe_deg[:])
-                    if last_pass and i == 3:
-                        nc.vector.scalar_tensor_tensor(
-                            out=inv_deg[:], in0=deg[:], scalar=0.0, in1=recip[:], op0=ALU.not_equal, op1=ALU.mult
-                        )
-
-                if last_pass:
-                    multiply(c)
-            finished = (h, acc, inv_deg)
-        scale_and_store(*finished, vector_helps=True)
+            if k + 1 < len(chunks):
+                degree_sums(*chunks[k + 1])
+            regroup(nc.vector.tensor_copy, grouped[(g, c)][:, :split, :], raw[(g, c)][:, :, :split])
+            short_steps()
+            regroup(nc.scalar.copy, grouped[(g, c)][:, split:, :], raw[(g, c)][:, :, split:])
+            if c == LAST and k + 1 < len(chunks):
+                start_chain(g)
+            if k == X_BEHIND:
+                nc.vector.quantize_mx(
+                    out=x_codes[:].rearrange("p c d -> p (c d)").bitcast(FP8X4),
+                    scales=x_scales[:].rearrange("p c d -> p (c d)"),
+                    in_=x_grouped[:].rearrange("p c d j -> p (c d j)"),
+                )
+                x_ready.append(True)
+                multiply()
+                short_steps()
+            if k == X_BEHIND - 1:
+                regroup_x()
+            if k + 2 == len(chunks):
+                start_chain(chunks[-1][0])
+            if k > 0:
+                quantize(*chunks[k - 1])
+            for t in [t for t in multiplied if t in scaled]:
+                multiplied.remove(t)
+                scale_and_store(t, on_vector=False)
+        quantize(*chunks[-1])
+        while any(done < len(steps) for steps, tiles, done in chains):
+            short_steps()
+        for i, t in enumerate(multiplied):
+            scale_and_store(t, on_vector=(i % 2 == 0))

@@ -190,6 +190,9 @@ def tile_v2emsgpass_s_kernel(tc, X, H, out):
             if k + 1 < len(chunks):
                 degree_sums(*chunks[k + 1])
             regroup(nc.vector.tensor_copy, grouped[(g, c)][:, :split, :], raw[(g, c)][:, :, :split])
+            if k == len(chunks) - 1:
+                start_chain(g)
+                short_steps()
             short_steps()
             regroup(nc.scalar.copy, grouped[(g, c)][:, split:, :], raw[(g, c)][:, :, split:])
             if c == LAST and k + 1 < len(chunks):
@@ -205,13 +208,14 @@ def tile_v2emsgpass_s_kernel(tc, X, H, out):
                 short_steps()
             if k == X_BEHIND - 1:
                 regroup_x()
-            if k + 2 == len(chunks):
-                start_chain(chunks[-1][0])
-            if k > 0:
+            if 0 < k < len(chunks) - 1:
                 quantize(*chunks[k - 1])
-            for t in [t for t in multiplied if t in scaled]:
-                multiplied.remove(t)
-                scale_and_store(t, on_vector=False)
+            if k == len(chunks) - 2:
+                quantize(g, c)
+            if k != len(chunks) - 2:
+                for t in [t for t in multiplied if t in scaled]:
+                    multiplied.remove(t)
+                    scale_and_store(t, on_vector=False)
         quantize(*chunks[-1])
         while any(done < len(steps) for steps, tiles, done in chains):
             short_steps()

@@ -180,6 +180,7 @@ def tile_v2emsgpass_s_kernel(tc, X, H, out):
         if X_BEHIND == 0:
             regroup_x()
         degree_sums(*chunks[0])
+        ripe = []
         for k, (g, c) in enumerate(chunks):
             width = GROUP_TILES[g] * E_TILE
             split = width * VECTOR_SHARE[0] // VECTOR_SHARE[1]
@@ -195,6 +196,9 @@ def tile_v2emsgpass_s_kernel(tc, X, H, out):
                 short_steps()
             short_steps()
             regroup(nc.scalar.copy, grouped[(g, c)][:, split:, :], raw[(g, c)][:, :, split:])
+            for t in ripe:
+                multiplied.remove(t)
+                scale_and_store(t, on_vector=False)
             if c == LAST and k + 1 < len(chunks):
                 start_chain(g)
             if k == X_BEHIND:
@@ -212,10 +216,7 @@ def tile_v2emsgpass_s_kernel(tc, X, H, out):
                 quantize(*chunks[k - 1])
             if k == len(chunks) - 2:
                 quantize(g, c)
-            if k != len(chunks) - 2:
-                for t in [t for t in multiplied if t in scaled]:
-                    multiplied.remove(t)
-                    scale_and_store(t, on_vector=False)
+            ripe = [t for t in multiplied if t in scaled]
         quantize(*chunks[-1])
         while any(done < len(steps) for steps, tiles, done in chains):
             short_steps()

@@ -21,11 +21,10 @@ PASSES = VERTICES // K_PASS
 LAST = PASSES - 1
 E_TILE = 128
 RUN = 4
-PSUM_BANKS = 8
-DEG_BANKS = 2
+CHAIN_GROUPS = ((0, 1), (2,))
+BANK_TILES = ((0, 1), (2, 4), (3, 5), (6,), (7,))
 GROUP_TILES = (2, 4, 2)
-VECTOR_SHARE = (8, 16)
-X_BEHIND = 0
+SHARERS = 2
 
 FLOPS = 2 * VERTICES * EDGES * FEATURES
 
@@ -41,8 +40,8 @@ def tile_v2emsgpass_s_kernel(tc, X, H, out):
     nc = tc.nc
     with ExitStack() as ctx:
         keep = ctx.enter_context(tc.tile_pool(name="keep", bufs=1))
-        deg_psum = ctx.enter_context(tc.psum_pool(name="deg_psum", bufs=DEG_BANKS))
-        acc_psum = ctx.enter_context(tc.psum_pool(name="acc_psum", bufs=PSUM_BANKS - DEG_BANKS))
+        deg_psum = ctx.enter_context(tc.psum_pool(name="deg_psum", bufs=1))
+        acc_psum = ctx.enter_context(tc.psum_pool(name="acc_psum", bufs=1))
         ctx.enter_context(tc.manual_schedule())
 
         chunks = [(g, c) for g in range(len(GROUP_TILES)) for c in range(PASSES)]
@@ -51,9 +50,8 @@ def tile_v2emsgpass_s_kernel(tc, X, H, out):
 
         x_raw = keep.tile([P, PASSES, PACK, FEATURES], BF16, name="x_raw")
         raw = {}
-        for k, (g, c) in enumerate(chunks):
-            if k == X_BEHIND:
-                nc.sync.dma_start(out=x_raw[:], in_=X.rearrange("(c p j) d -> p c j d", c=PASSES, j=PACK))
+        nc.sync.dma_start(out=x_raw[:], in_=X.rearrange("(c p j) d -> p c j d", c=PASSES, j=PACK))
+        for g, c in chunks:
             width = GROUP_TILES[g] * E_TILE
             raw[(g, c)] = keep.tile([P, PACK, width], BF16, name="raw_%d_%d" % (g, c))
             nc.sync.dma_start(
@@ -72,7 +70,24 @@ def tile_v2emsgpass_s_kernel(tc, X, H, out):
         x_codes = keep.tile([P, PASSES, FEATURES], U32, name="x_codes", align_bytes=64)
         x_scales = keep.tile([P, PASSES, FEATURES], U8, name="x_scales", align_bytes=64)
 
+        acc = {}
+        second = set()
+        for b, tiles in enumerate(BANK_TILES):
+            bank = acc_psum.tile([P, len(tiles), FEATURES], F32, name="acc_%d" % b)
+            for slot, t in enumerate(tiles):
+                acc[t] = bank[:, slot, :]
+                if slot > 0:
+                    second.add(t)
         deg_ps = {}
+        deg_slot = {}
+        chain_tiles = {}
+        for n, groups in enumerate(CHAIN_GROUPS):
+            tiles = [first_tile[g] + i for g in groups for i in range(GROUP_TILES[g])]
+            sums = deg_psum.tile([P, PASSES, len(tiles)], F32, name="deg_ps_%d" % n)
+            chain_tiles[groups[-1]] = tiles
+            for slot, t in enumerate(tiles):
+                deg_ps[t] = sums
+                deg_slot[t] = slot
         deg = keep.tile([P, tiles_in_all], F32, name="deg")
         safe_deg = keep.tile([P, tiles_in_all], F32, name="safe_deg")
         recip = keep.tile([P, tiles_in_all], F32, name="recip")
@@ -81,30 +96,27 @@ def tile_v2emsgpass_s_kernel(tc, X, H, out):
         grouped = {}
         codes = {}
         scales = {}
-        acc = {}
         chains = []
         scaled = set()
         quantised = []
         multiplied = []
-        x_ready = []
 
         def degree_sums(g, c):
-            if c == 0:
-                deg_ps[g] = deg_psum.tile([P, PASSES, GROUP_TILES[g]], F32, name="deg_ps")
             for i in range(GROUP_TILES[g]):
+                t = first_tile[g] + i
                 for j in range(PACK):
                     nc.tensor.matmul(
-                        out=deg_ps[g][:, c, i : i + 1],
+                        out=deg_ps[t][:, c, deg_slot[t] : deg_slot[t] + 1],
                         lhsT=raw[(g, c)][:, j, i * E_TILE : (i + 1) * E_TILE],
                         rhs=ones[:],
                         start=(j == 0),
                         stop=(j == PACK - 1),
                     )
 
-        def reciprocal_steps(g, cols):
+        def reciprocal_steps(sums, cols):
             return [
                 lambda: nc.vector.tensor_reduce(
-                    out=deg[:, cols], in_=deg_ps[g][:].rearrange("p c t -> p t c"), axis=AXIS.X, op=ALU.add
+                    out=deg[:, cols], in_=sums[:].rearrange("p c t -> p t c"), axis=AXIS.X, op=ALU.add
                 ),
                 lambda: nc.vector.scalar_tensor_tensor(
                     out=safe_deg[:, cols], in0=deg[:, cols], scalar=0.0, in1=deg[:, cols],
@@ -118,8 +130,9 @@ def tile_v2emsgpass_s_kernel(tc, X, H, out):
             ]
 
         def start_chain(g):
-            tiles = list(range(first_tile[g], first_tile[g] + GROUP_TILES[g]))
-            chains.append([reciprocal_steps(g, slice(tiles[0], tiles[-1] + 1)), tiles, 0])
+            if g in chain_tiles:
+                tiles = chain_tiles[g]
+                chains.append([reciprocal_steps(deg_ps[tiles[0]], slice(tiles[0], tiles[-1] + 1)), tiles, 0])
 
         def short_steps():
             for chain in chains:
@@ -132,93 +145,99 @@ def tile_v2emsgpass_s_kernel(tc, X, H, out):
                             scaled.add(t)
 
         def multiply():
-            if not x_ready:
-                return
-            for g, c in quantised:
-                for i in range(GROUP_TILES[g]):
-                    if c == 0:
-                        acc_t = acc_psum.tile([P, FEATURES], F32, name="acc")
-                        acc[first_tile[g] + i] = acc_t
-                    nc.tensor.matmul_mx(
-                        out=acc[first_tile[g] + i][:],
-                        lhsT=codes[(g, c)][:, i * E_TILE : (i + 1) * E_TILE].bitcast(FP8X4),
-                        lhsT_scale=scales[(g, c)][:, i * E_TILE : (i + 1) * E_TILE],
-                        rhs=x_codes[:, c, :].bitcast(FP8X4),
-                        rhs_scale=x_scales[:, c, :],
-                        start=(c == 0),
-                        stop=(c == LAST),
-                    )
-                    if c == LAST:
-                        multiplied.append(first_tile[g] + i)
+            for g, c, part in quantised:
+                for late in (False, True):
+                    for i in part:
+                        t = first_tile[g] + i
+                        if (t in second) != late or (late and c < LAST):
+                            continue
+                        for cm in range(PASSES) if late else (c,):
+                            nc.tensor.matmul_mx(
+                                out=acc[t],
+                                lhsT=codes[(g, cm)][:, i * E_TILE : (i + 1) * E_TILE].bitcast(FP8X4),
+                                lhsT_scale=scales[(g, cm)][:, i * E_TILE : (i + 1) * E_TILE],
+                                rhs=x_codes[:, cm, :].bitcast(FP8X4),
+                                rhs_scale=x_scales[:, cm, :],
+                                start=(cm == 0),
+                                stop=(cm == LAST),
+                            )
+                        if c == LAST:
+                            multiplied.append(t)
             quantised.clear()
 
-        def quantize(g, c):
+        def quantize(g, c, half):
+            part = GROUP_TILES[g] // SHARERS
+            tiles = range(half * part, (half + 1) * part)
+            cols = slice(tiles[0] * E_TILE, (tiles[-1] + 1) * E_TILE)
             nc.vector.quantize_mx(
-                out=codes[(g, c)][:].bitcast(FP8X4),
-                scales=scales[(g, c)][:],
-                in_=grouped[(g, c)][:].rearrange("p w j -> p (w j)"),
+                out=codes[(g, c)][:, cols].bitcast(FP8X4),
+                scales=scales[(g, c)][:, cols],
+                in_=grouped[(g, c)][:, cols, :].rearrange("p w j -> p (w j)"),
             )
-            quantised.append((g, c))
-            multiply()
-            short_steps()
+            quantised.append((g, c, tiles))
 
         def scale_and_store(t, on_vector):
             res = keep.tile([P, FEATURES], F32, name="res_%d" % t)
             if on_vector:
                 nc.vector.tensor_scalar(
-                    out=res[:], in0=acc[t][:], scalar1=inv_deg[:, t : t + 1], scalar2=None, op0=ALU.mult
+                    out=res[:], in0=acc[t], scalar1=inv_deg[:, t : t + 1], scalar2=None, op0=ALU.mult
                 )
             else:
-                nc.scalar.activation(out=res[:], in_=acc[t][:], func=ACT.Copy, scale=inv_deg[:, t : t + 1])
+                nc.scalar.activation(out=res[:], in_=acc[t], func=ACT.Copy, scale=inv_deg[:, t : t + 1])
             nc.sync.dma_start(out=out[t * E_TILE : (t + 1) * E_TILE, :], in_=res[:])
 
-        def regroup_x():
-            for cx in range(PASSES):
-                regroup(nc.vector.tensor_copy, x_grouped[:, cx], x_raw[:, cx])
-                short_steps()
+        def quantize_x():
+            nc.vector.quantize_mx(
+                out=x_codes[:].rearrange("p c d -> p (c d)").bitcast(FP8X4),
+                scales=x_scales[:].rearrange("p c d -> p (c d)"),
+                in_=x_grouped[:].rearrange("p c d j -> p (c d j)"),
+            )
 
-        if X_BEHIND == 0:
-            regroup_x()
+        def regroup_x():
+            regroup(nc.vector.tensor_copy, x_grouped[:, 0], x_raw[:, 0])
+            regroup(nc.scalar.copy, x_grouped[:, 1], x_raw[:, 1])
+
+        regroup_x()
         degree_sums(*chunks[0])
-        ripe = []
         for k, (g, c) in enumerate(chunks):
             width = GROUP_TILES[g] * E_TILE
-            split = width * VECTOR_SHARE[0] // VECTOR_SHARE[1]
+            split = width // SHARERS
+            last = k == len(chunks) - 1
             grouped[(g, c)] = keep.tile([P, width, PACK], BF16, name="grouped_%d_%d" % (g, c), align_bytes=64)
             codes[(g, c)] = keep.tile([P, width], U32, name="codes_%d_%d" % (g, c), align_bytes=64)
             scales[(g, c)] = keep.tile([P, width], U8, name="scales_%d_%d" % (g, c), align_bytes=64)
 
-            if k + 1 < len(chunks):
+            if not last:
                 degree_sums(*chunks[k + 1])
-            regroup(nc.vector.tensor_copy, grouped[(g, c)][:, :split, :], raw[(g, c)][:, :, :split])
-            if k == len(chunks) - 1:
+            else:
                 start_chain(g)
                 short_steps()
+            regroup(nc.vector.tensor_copy, grouped[(g, c)][:, :split, :], raw[(g, c)][:, :, :split])
             short_steps()
             regroup(nc.scalar.copy, grouped[(g, c)][:, split:, :], raw[(g, c)][:, :, split:])
-            for t in ripe:
-                multiplied.remove(t)
-                scale_and_store(t, on_vector=False)
-            if c == LAST and k + 1 < len(chunks):
-                start_chain(g)
-            if k == X_BEHIND:
-                nc.vector.quantize_mx(
-                    out=x_codes[:].rearrange("p c d -> p (c d)").bitcast(FP8X4),
-                    scales=x_scales[:].rearrange("p c d -> p (c d)"),
-                    in_=x_grouped[:].rearrange("p c d j -> p (c d j)"),
-                )
-                x_ready.append(True)
-                multiply()
-                short_steps()
-            if k == X_BEHIND - 1:
-                regroup_x()
-            if 0 < k < len(chunks) - 1:
-                quantize(*chunks[k - 1])
+            if last:
+                for t in list(multiplied):
+                    multiplied.remove(t)
+                    scale_and_store(t, on_vector=False)
+            if k == 0:
+                quantize_x()
+            elif k < len(chunks) - 2:
+                quantize(*chunks[k - 1], 1)
             if k == len(chunks) - 2:
-                quantize(g, c)
-            ripe = [t for t in multiplied if t in scaled]
-        quantize(*chunks[-1])
-        while any(done < len(steps) for steps, tiles, done in chains):
+                quantize(*chunks[k - 1], 1)
+                short_steps()
+            if not last:
+                quantize(g, c, 0)
+                multiply()
+                if c == LAST:
+                    start_chain(g)
+                short_steps()
+            if k == len(chunks) - 2:
+                quantize(g, c, 1)
+                multiply()
+        for half in reversed(range(SHARERS)):
+            quantize(*chunks[-1], half)
+            multiply()
             short_steps()
         for i, t in enumerate(multiplied):
             scale_and_store(t, on_vector=(i % 2 == 0))

@@ -25,6 +25,7 @@ CHAIN_GROUPS = ((0, 1), (2,))
 BANK_TILES = ((0, 1), (2, 4), (3, 5), (6,), (7,))
 GROUP_TILES = (2, 4, 2)
 SHARERS = 2
+FILL = 256
 
 FLOPS = 2 * VERTICES * EDGES * FEATURES
 
@@ -63,6 +64,26 @@ def tile_v2emsgpass_s_kernel(tc, X, H, out):
 
         ones = keep.tile([P, 1], BF16, name="ones")
         nc.vector.memset(ones[:], 1.0)
+        fill = keep.tile([P, FILL * PACK], BF16, name="fill", align_bytes=64)
+        fill_codes = keep.tile([P, FILL], U32, name="fill_codes", align_bytes=64)
+        fill_scales = keep.tile([P, FILL], U8, name="fill_scales", align_bytes=64)
+        nc.gpsimd.memset(fill[:], 1.0)
+        nc.vector.quantize_mx(out=fill_codes[:].bitcast(FP8X4), scales=fill_scales[:], in_=fill[:])
+        fill_psum = ctx.enter_context(tc.psum_pool(name="fill_psum", bufs=1))
+        fill_acc = fill_psum.tile([P, FILL], F32, name="fill_acc")
+
+        def filler(passes):
+            for n in range(passes):
+                nc.tensor.matmul_mx(
+                    out=fill_acc[:],
+                    lhsT=fill_codes[:, :E_TILE].bitcast(FP8X4),
+                    lhsT_scale=fill_scales[:, :E_TILE],
+                    rhs=fill_codes[:].bitcast(FP8X4),
+                    rhs_scale=fill_scales[:],
+                    start=True,
+                    stop=True,
+                )
+
         table_warm = keep.tile([P, 1], F32, name="table_warm")
         nc.scalar.activation(out=table_warm[:], in_=ones[:], func=ACT.Copy)
 
@@ -198,6 +219,7 @@ def tile_v2emsgpass_s_kernel(tc, X, H, out):
             regroup(nc.scalar.copy, x_grouped[:, 1], x_raw[:, 1])
 
         regroup_x()
+        filler(7)
         degree_sums(*chunks[0])
         for k, (g, c) in enumerate(chunks):
             width = GROUP_TILES[g] * E_TILE
@@ -208,6 +230,7 @@ def tile_v2emsgpass_s_kernel(tc, X, H, out):
             scales[(g, c)] = keep.tile([P, width], U8, name="scales_%d_%d" % (g, c), align_bytes=64)
 
             if not last:
+                filler(1)
                 degree_sums(*chunks[k + 1])
             else:
                 start_chain(g)

@@ -21,11 +21,14 @@ PASSES = VERTICES // K_PASS
 LAST = PASSES - 1
 E_TILE = 128
 RUN = 4
-CHAIN_GROUPS = ((0, 1), (2,))
+CHAIN_GROUPS = ((0,), (1,), (2,))
 BANK_TILES = ((0, 1), (2, 4), (3, 5), (6,), (7,))
 GROUP_TILES = (2, 4, 2)
 SHARERS = 2
+VECTOR_SHARE = (8, 8, 8, 8, 9, 8)
+BANK_SLOTS = 2
 FILL = 256
+WHOLE = (1, 4)
 
 FLOPS = 2 * VERTICES * EDGES * FEATURES
 
@@ -69,21 +72,6 @@ def tile_v2emsgpass_s_kernel(tc, X, H, out):
         fill_scales = keep.tile([P, FILL], U8, name="fill_scales", align_bytes=64)
         nc.gpsimd.memset(fill[:], 1.0)
         nc.vector.quantize_mx(out=fill_codes[:].bitcast(FP8X4), scales=fill_scales[:], in_=fill[:])
-        fill_psum = ctx.enter_context(tc.psum_pool(name="fill_psum", bufs=1))
-        fill_acc = fill_psum.tile([P, FILL], F32, name="fill_acc")
-
-        def filler(passes):
-            for n in range(passes):
-                nc.tensor.matmul_mx(
-                    out=fill_acc[:],
-                    lhsT=fill_codes[:, :E_TILE].bitcast(FP8X4),
-                    lhsT_scale=fill_scales[:, :E_TILE],
-                    rhs=fill_codes[:].bitcast(FP8X4),
-                    rhs_scale=fill_scales[:],
-                    start=True,
-                    stop=True,
-                )
-
         table_warm = keep.tile([P, 1], F32, name="table_warm")
         nc.scalar.activation(out=table_warm[:], in_=ones[:], func=ACT.Copy)
 
@@ -92,11 +80,13 @@ def tile_v2emsgpass_s_kernel(tc, X, H, out):
         x_scales = keep.tile([P, PASSES, FEATURES], U8, name="x_scales", align_bytes=64)
 
         acc = {}
+        banks = {}
         second = set()
         for b, tiles in enumerate(BANK_TILES):
-            bank = acc_psum.tile([P, len(tiles), FEATURES], F32, name="acc_%d" % b)
+            bank = acc_psum.tile([P, BANK_SLOTS * FEATURES], F32, name="acc_%d" % b)
             for slot, t in enumerate(tiles):
-                acc[t] = bank[:, slot, :]
+                acc[t] = bank[:, slot * FEATURES : (slot + 1) * FEATURES]
+                banks[t] = bank
                 if slot > 0:
                     second.add(t)
         deg_ps = {}
@@ -207,6 +197,18 @@ def tile_v2emsgpass_s_kernel(tc, X, H, out):
                 nc.scalar.activation(out=res[:], in_=acc[t], func=ACT.Copy, scale=inv_deg[:, t : t + 1])
             nc.sync.dma_start(out=out[t * E_TILE : (t + 1) * E_TILE, :], in_=res[:])
 
+        def filler(passes):
+            for n in range(passes):
+                nc.tensor.matmul_mx(
+                    out=banks[tiles_in_all - 1][:, :FILL],
+                    lhsT=fill_codes[:, :E_TILE].bitcast(FP8X4),
+                    lhsT_scale=fill_scales[:, :E_TILE],
+                    rhs=fill_codes[:].bitcast(FP8X4),
+                    rhs_scale=fill_scales[:],
+                    start=True,
+                    stop=True,
+                )
+
         def quantize_x():
             nc.vector.quantize_mx(
                 out=x_codes[:].rearrange("p c d -> p (c d)").bitcast(FP8X4),
@@ -223,14 +225,15 @@ def tile_v2emsgpass_s_kernel(tc, X, H, out):
         degree_sums(*chunks[0])
         for k, (g, c) in enumerate(chunks):
             width = GROUP_TILES[g] * E_TILE
-            split = width // SHARERS
+            split = width * VECTOR_SHARE[k] // 16
             last = k == len(chunks) - 1
             grouped[(g, c)] = keep.tile([P, width, PACK], BF16, name="grouped_%d_%d" % (g, c), align_bytes=64)
             codes[(g, c)] = keep.tile([P, width], U32, name="codes_%d_%d" % (g, c), align_bytes=64)
             scales[(g, c)] = keep.tile([P, width], U8, name="scales_%d_%d" % (g, c), align_bytes=64)
 
             if not last:
-                filler(1)
+                if k < 2:
+                    filler(1)
                 degree_sums(*chunks[k + 1])
             else:
                 start_chain(g)
@@ -238,15 +241,12 @@ def tile_v2emsgpass_s_kernel(tc, X, H, out):
             regroup(nc.vector.tensor_copy, grouped[(g, c)][:, :split, :], raw[(g, c)][:, :, :split])
             short_steps()
             regroup(nc.scalar.copy, grouped[(g, c)][:, split:, :], raw[(g, c)][:, :, split:])
-            if last:
-                for t in list(multiplied):
-                    multiplied.remove(t)
-                    scale_and_store(t, on_vector=False)
+            for t in [t for t in multiplied if t in scaled and k >= len(chunks) - 2]:
+                multiplied.remove(t)
+                scale_and_store(t, on_vector=False)
             if k == 0:
                 quantize_x()
-            elif k < len(chunks) - 2:
-                quantize(*chunks[k - 1], 1)
-            if k == len(chunks) - 2:
+            elif k - 1 not in WHOLE:
                 quantize(*chunks[k - 1], 1)
                 short_steps()
             if not last:
@@ -255,9 +255,10 @@ def tile_v2emsgpass_s_kernel(tc, X, H, out):
                 if c == LAST:
                     start_chain(g)
                 short_steps()
-            if k == len(chunks) - 2:
-                quantize(g, c, 1)
-                multiply()
+                if k in WHOLE:
+                    quantize(g, c, 1)
+                    multiply()
+                    short_steps()
         for half in reversed(range(SHARERS)):
             quantize(*chunks[-1], half)
             multiply()

@@ -25,7 +25,7 @@ CHAIN_GROUPS = ((0,), (1,), (2,))
 BANK_TILES = ((0, 1), (2, 4), (3, 5), (6,), (7,))
 GROUP_TILES = (2, 4, 2)
 SHARERS = 2
-VECTOR_SHARE = (8, 8, 8, 8, 9, 8)
+VECTOR_SHARE = (8, 8, 8, 9, 8, 8)
 BANK_SLOTS = 2
 FILL = 256
 WHOLE = (1, 4)
@@ -176,9 +176,9 @@ def tile_v2emsgpass_s_kernel(tc, X, H, out):
                             multiplied.append(t)
             quantised.clear()
 
-        def quantize(g, c, half):
+        def quantize(g, c, first, halves=1):
             part = GROUP_TILES[g] // SHARERS
-            tiles = range(half * part, (half + 1) * part)
+            tiles = range(first * part, (first + halves) * part)
             cols = slice(tiles[0] * E_TILE, (tiles[-1] + 1) * E_TILE)
             nc.vector.quantize_mx(
                 out=codes[(g, c)][:, cols].bitcast(FP8X4),
@@ -234,7 +234,8 @@ def tile_v2emsgpass_s_kernel(tc, X, H, out):
             if not last:
                 if k < 2:
                     filler(1)
-                degree_sums(*chunks[k + 1])
+                if k + 1 < len(chunks) - 1:
+                    degree_sums(*chunks[k + 1])
             else:
                 start_chain(g)
                 short_steps()
@@ -249,7 +250,17 @@ def tile_v2emsgpass_s_kernel(tc, X, H, out):
             elif k - 1 not in WHOLE:
                 quantize(*chunks[k - 1], 1)
                 short_steps()
-            if not last:
+            if k == len(chunks) - 3:
+                quantize(g, c, 0)
+                degree_sums(*chunks[-1])
+                multiply()
+                start_chain(g)
+                short_steps()
+            elif k == len(chunks) - 2:
+                quantize(g, c, 0, SHARERS)
+                multiply()
+                short_steps()
+            elif not last:
                 quantize(g, c, 0)
                 multiply()
                 if c == LAST:
@@ -263,5 +274,5 @@ def tile_v2emsgpass_s_kernel(tc, X, H, out):
             quantize(*chunks[-1], half)
             multiply()
             short_steps()
-        for i, t in enumerate(multiplied):
-            scale_and_store(t, on_vector=(i % 2 == 0))
+        for t in multiplied:
+            scale_and_store(t, on_vector=True)

@@ -21,14 +21,12 @@ PASSES = VERTICES // K_PASS
 LAST = PASSES - 1
 E_TILE = 128
 RUN = 4
-CHAIN_GROUPS = ((0,), (1,), (2,))
-BANK_TILES = ((0, 1), (2, 4), (3, 5), (6,), (7,))
-GROUP_TILES = (2, 4, 2)
-SHARERS = 2
-VECTOR_SHARE = (8, 8, 8, 9, 8, 8)
-BANK_SLOTS = 2
+GROUP = 4
+GROUPS = EDGES // E_TILE // GROUP
+CHUNKS = [(g, c) for g in range(GROUPS) for c in range(PASSES)]
+VECTOR_SHARE = (8, 8, 8, 9)
+HALF = GROUP // 2
 FILL = 256
-WHOLE = (1, 4)
 
 FLOPS = 2 * VERTICES * EDGES * FEATURES
 
@@ -44,163 +42,76 @@ def tile_v2emsgpass_s_kernel(tc, X, H, out):
     nc = tc.nc
     with ExitStack() as ctx:
         keep = ctx.enter_context(tc.tile_pool(name="keep", bufs=1))
-        deg_psum = ctx.enter_context(tc.psum_pool(name="deg_psum", bufs=1))
-        acc_psum = ctx.enter_context(tc.psum_pool(name="acc_psum", bufs=1))
+        psum = ctx.enter_context(tc.psum_pool(name="psum", bufs=1))
         ctx.enter_context(tc.manual_schedule())
 
-        chunks = [(g, c) for g in range(len(GROUP_TILES)) for c in range(PASSES)]
-        first_tile = [sum(GROUP_TILES[:g]) for g in range(len(GROUP_TILES))]
-        tiles_in_all = sum(GROUP_TILES)
-
-        x_raw = keep.tile([P, PASSES, PACK, FEATURES], BF16, name="x_raw")
         raw = {}
-        nc.sync.dma_start(out=x_raw[:], in_=X.rearrange("(c p j) d -> p c j d", c=PASSES, j=PACK))
-        for g, c in chunks:
-            width = GROUP_TILES[g] * E_TILE
-            raw[(g, c)] = keep.tile([P, PACK, width], BF16, name="raw_%d_%d" % (g, c))
+        x_raw = keep.tile([P, PASSES, PACK, FEATURES], BF16, name="x_raw")
+
+        def load_x():
+            nc.sync.dma_start(out=x_raw[:], in_=X.rearrange("(c p j) d -> p c j d", c=PASSES, j=PACK))
+
+        def load(g, c):
+            raw[(g, c)] = keep.tile([P, PACK, GROUP * E_TILE], BF16, name="raw_%d_%d" % (g, c))
             nc.sync.dma_start(
                 out=raw[(g, c)][:],
                 in_=H[
-                    c * K_PASS : (c + 1) * K_PASS, first_tile[g] * E_TILE : first_tile[g] * E_TILE + width
+                    c * K_PASS : (c + 1) * K_PASS, g * GROUP * E_TILE : (g + 1) * GROUP * E_TILE
                 ].rearrange("(p j) e -> p j e", j=PACK),
             )
 
+        load_x()
+        for g, c in CHUNKS:
+            load(g, c)
+
         ones = keep.tile([P, 1], BF16, name="ones")
         nc.vector.memset(ones[:], 1.0)
+        table_warm = keep.tile([P, 1], F32, name="table_warm")
+        nc.scalar.activation(out=table_warm[:], in_=ones[:], func=ACT.Copy)
         fill = keep.tile([P, FILL * PACK], BF16, name="fill", align_bytes=64)
         fill_codes = keep.tile([P, FILL], U32, name="fill_codes", align_bytes=64)
         fill_scales = keep.tile([P, FILL], U8, name="fill_scales", align_bytes=64)
         nc.gpsimd.memset(fill[:], 1.0)
         nc.vector.quantize_mx(out=fill_codes[:].bitcast(FP8X4), scales=fill_scales[:], in_=fill[:])
-        table_warm = keep.tile([P, 1], F32, name="table_warm")
-        nc.scalar.activation(out=table_warm[:], in_=ones[:], func=ACT.Copy)
 
         x_grouped = keep.tile([P, PASSES, FEATURES, PACK], BF16, name="x_grouped", align_bytes=64)
         x_codes = keep.tile([P, PASSES, FEATURES], U32, name="x_codes", align_bytes=64)
         x_scales = keep.tile([P, PASSES, FEATURES], U8, name="x_scales", align_bytes=64)
-
-        acc = {}
-        banks = {}
-        second = set()
-        for b, tiles in enumerate(BANK_TILES):
-            bank = acc_psum.tile([P, BANK_SLOTS * FEATURES], F32, name="acc_%d" % b)
-            for slot, t in enumerate(tiles):
-                acc[t] = bank[:, slot * FEATURES : (slot + 1) * FEATURES]
-                banks[t] = bank
-                if slot > 0:
-                    second.add(t)
-        deg_ps = {}
-        deg_slot = {}
-        chain_tiles = {}
-        for n, groups in enumerate(CHAIN_GROUPS):
-            tiles = [first_tile[g] + i for g in groups for i in range(GROUP_TILES[g])]
-            sums = deg_psum.tile([P, PASSES, len(tiles)], F32, name="deg_ps_%d" % n)
-            chain_tiles[groups[-1]] = tiles
-            for slot, t in enumerate(tiles):
-                deg_ps[t] = sums
-                deg_slot[t] = slot
-        deg = keep.tile([P, tiles_in_all], F32, name="deg")
-        safe_deg = keep.tile([P, tiles_in_all], F32, name="safe_deg")
-        recip = keep.tile([P, tiles_in_all], F32, name="recip")
-        inv_deg = keep.tile([P, tiles_in_all], F32, name="inv_deg")
-
         grouped = {}
         codes = {}
         scales = {}
-        chains = []
-        scaled = set()
-        quantised = []
-        multiplied = []
+        for g, c in CHUNKS:
+            width = GROUP * E_TILE
+            grouped[(g, c)] = keep.tile([P, width, PACK], BF16, name="grouped_%d_%d" % (g, c), align_bytes=64)
+            codes[(g, c)] = keep.tile([P, width], U32, name="codes_%d_%d" % (g, c), align_bytes=64)
+            scales[(g, c)] = keep.tile([P, width], U8, name="scales_%d_%d" % (g, c), align_bytes=64)
 
-        def degree_sums(g, c):
-            for i in range(GROUP_TILES[g]):
-                t = first_tile[g] + i
-                for j in range(PACK):
-                    nc.tensor.matmul(
-                        out=deg_ps[t][:, c, deg_slot[t] : deg_slot[t] + 1],
-                        lhsT=raw[(g, c)][:, j, i * E_TILE : (i + 1) * E_TILE],
-                        rhs=ones[:],
-                        start=(j == 0),
-                        stop=(j == PACK - 1),
-                    )
-
-        def reciprocal_steps(sums, cols):
-            return [
-                lambda: nc.vector.tensor_reduce(
-                    out=deg[:, cols], in_=sums[:].rearrange("p c t -> p t c"), axis=AXIS.X, op=ALU.add
-                ),
-                lambda: nc.vector.scalar_tensor_tensor(
-                    out=safe_deg[:, cols], in0=deg[:, cols], scalar=0.0, in1=deg[:, cols],
-                    op0=ALU.is_equal, op1=ALU.add,
-                ),
-                lambda: nc.vector.reciprocal(out=recip[:, cols], in_=safe_deg[:, cols]),
-                lambda: nc.vector.scalar_tensor_tensor(
-                    out=inv_deg[:, cols], in0=deg[:, cols], scalar=0.0, in1=recip[:, cols],
-                    op0=ALU.not_equal, op1=ALU.mult,
-                ),
-            ]
-
-        def start_chain(g):
-            if g in chain_tiles:
-                tiles = chain_tiles[g]
-                chains.append([reciprocal_steps(deg_ps[tiles[0]], slice(tiles[0], tiles[-1] + 1)), tiles, 0])
-
-        def short_steps():
-            for chain in chains:
-                steps, tiles, done = chain
-                if done < len(steps):
-                    steps[done]()
-                    chain[2] = done + 1
-                    if chain[2] == len(steps):
-                        for t in tiles:
-                            scaled.add(t)
-
-        def multiply():
-            for g, c, part in quantised:
-                for late in (False, True):
-                    for i in part:
-                        t = first_tile[g] + i
-                        if (t in second) != late or (late and c < LAST):
-                            continue
-                        for cm in range(PASSES) if late else (c,):
-                            nc.tensor.matmul_mx(
-                                out=acc[t],
-                                lhsT=codes[(g, cm)][:, i * E_TILE : (i + 1) * E_TILE].bitcast(FP8X4),
-                                lhsT_scale=scales[(g, cm)][:, i * E_TILE : (i + 1) * E_TILE],
-                                rhs=x_codes[:, cm, :].bitcast(FP8X4),
-                                rhs_scale=x_scales[:, cm, :],
-                                start=(cm == 0),
-                                stop=(cm == LAST),
-                            )
-                        if c == LAST:
-                            multiplied.append(t)
-            quantised.clear()
-
-        def quantize(g, c, first, halves=1):
-            part = GROUP_TILES[g] // SHARERS
-            tiles = range(first * part, (first + halves) * part)
-            cols = slice(tiles[0] * E_TILE, (tiles[-1] + 1) * E_TILE)
-            nc.vector.quantize_mx(
-                out=codes[(g, c)][:, cols].bitcast(FP8X4),
-                scales=scales[(g, c)][:, cols],
-                in_=grouped[(g, c)][:, cols, :].rearrange("p w j -> p (w j)"),
-            )
-            quantised.append((g, c, tiles))
-
-        def scale_and_store(t, on_vector):
-            res = keep.tile([P, FEATURES], F32, name="res_%d" % t)
-            if on_vector:
-                nc.vector.tensor_scalar(
-                    out=res[:], in0=acc[t], scalar1=inv_deg[:, t : t + 1], scalar2=None, op0=ALU.mult
-                )
-            else:
-                nc.scalar.activation(out=res[:], in_=acc[t], func=ACT.Copy, scale=inv_deg[:, t : t + 1])
-            nc.sync.dma_start(out=out[t * E_TILE : (t + 1) * E_TILE, :], in_=res[:])
+        deg_sums = {}
+        for g in range(GROUPS):
+            deg_sums[g] = psum.tile([P, PASSES, GROUP], F32, name="deg_sums_%d" % g)
+        products = {}
+        for i in range(HALF):
+            shared = psum.tile([P, 2 * FEATURES], F32, name="shared_%d" % i)
+            products[(0, i)] = shared[:, :FEATURES]
+            products[(0, HALF + i)] = shared[:, FEATURES:]
+        bank = {}
+        for i in range(GROUP):
+            bank[i] = psum.tile([P, 2 * FEATURES], F32, name="bank_%d" % i)
+            products[(1, i)] = bank[i][:, :FEATURES]
+        deg = {}
+        safe_deg = {}
+        recip = {}
+        inv_deg = {}
+        for g in range(GROUPS):
+            deg[g] = keep.tile([P, GROUP], F32, name="deg_%d" % g)
+            safe_deg[g] = keep.tile([P, GROUP], F32, name="safe_deg_%d" % g)
+            recip[g] = keep.tile([P, GROUP], F32, name="recip_%d" % g)
+            inv_deg[g] = keep.tile([P, GROUP], F32, name="inv_deg_%d" % g)
 
         def filler(passes):
             for n in range(passes):
                 nc.tensor.matmul_mx(
-                    out=banks[tiles_in_all - 1][:, :FILL],
+                    out=bank[GROUP - 1][:, :FILL],
                     lhsT=fill_codes[:, :E_TILE].bitcast(FP8X4),
                     lhsT_scale=fill_scales[:, :E_TILE],
                     rhs=fill_codes[:].bitcast(FP8X4),
@@ -209,6 +120,21 @@ def tile_v2emsgpass_s_kernel(tc, X, H, out):
                     stop=True,
                 )
 
+        def degree_sums(g, c):
+            for i in range(GROUP):
+                for j in range(PACK):
+                    nc.tensor.matmul(
+                        out=deg_sums[g][:, c, i : i + 1],
+                        lhsT=raw[(g, c)][:, j, i * E_TILE : (i + 1) * E_TILE],
+                        rhs=ones[:],
+                        start=(j == 0),
+                        stop=(j == PACK - 1),
+                    )
+
+        def regroup_x():
+            regroup(nc.vector.tensor_copy, x_grouped[:, 0], x_raw[:, 0])
+            regroup(nc.scalar.copy, x_grouped[:, 1], x_raw[:, 1])
+
         def quantize_x():
             nc.vector.quantize_mx(
                 out=x_codes[:].rearrange("p c d -> p (c d)").bitcast(FP8X4),
@@ -216,63 +142,113 @@ def tile_v2emsgpass_s_kernel(tc, X, H, out):
                 in_=x_grouped[:].rearrange("p c d j -> p (c d j)"),
             )
 
-        def regroup_x():
-            regroup(nc.vector.tensor_copy, x_grouped[:, 0], x_raw[:, 0])
-            regroup(nc.scalar.copy, x_grouped[:, 1], x_raw[:, 1])
+        def regroup_h(g, c):
+            split = GROUP * E_TILE * VECTOR_SHARE[CHUNKS.index((g, c))] // 16
+            regroup(nc.vector.tensor_copy, grouped[(g, c)][:, :split, :], raw[(g, c)][:, :, :split])
+            regroup(nc.scalar.copy, grouped[(g, c)][:, split:, :], raw[(g, c)][:, :, split:])
+
+        def quantize(g, c, tiles):
+            cols = slice(tiles[0] * E_TILE, (tiles[-1] + 1) * E_TILE)
+            nc.vector.quantize_mx(
+                out=codes[(g, c)][:, cols].bitcast(FP8X4),
+                scales=scales[(g, c)][:, cols],
+                in_=grouped[(g, c)][:, cols, :].rearrange("p w j -> p (w j)"),
+            )
+
+        def multiply(g, c, i):
+            nc.tensor.matmul_mx(
+                out=products[(g, i)],
+                lhsT=codes[(g, c)][:, i * E_TILE : (i + 1) * E_TILE].bitcast(FP8X4),
+                lhsT_scale=scales[(g, c)][:, i * E_TILE : (i + 1) * E_TILE],
+                rhs=x_codes[:, c, :].bitcast(FP8X4),
+                rhs_scale=x_scales[:, c, :],
+                start=(c == 0),
+                stop=(c == LAST),
+            )
+
+        def sum_passes(g):
+            nc.vector.tensor_reduce(
+                out=deg[g][:], in_=deg_sums[g][:].rearrange("p c t -> p t c"), axis=AXIS.X, op=ALU.add
+            )
+
+        def make_safe(g):
+            nc.vector.scalar_tensor_tensor(
+                out=safe_deg[g][:], in0=deg[g][:], scalar=0.0, in1=deg[g][:], op0=ALU.is_equal, op1=ALU.add
+            )
+
+        def invert(g):
+            nc.vector.reciprocal(out=recip[g][:], in_=safe_deg[g][:])
+
+        def mask(g):
+            nc.vector.scalar_tensor_tensor(
+                out=inv_deg[g][:], in0=deg[g][:], scalar=0.0, in1=recip[g][:], op0=ALU.not_equal, op1=ALU.mult
+            )
+
+        def scale_and_store(g, i, on_vector):
+            t = g * GROUP + i
+            res = keep.tile([P, FEATURES], F32, name="res_%d" % t)
+            if on_vector:
+                nc.vector.tensor_scalar(
+                    out=res[:], in0=products[(g, i)], scalar1=inv_deg[g][:, i : i + 1], scalar2=None, op0=ALU.mult
+                )
+            else:
+                nc.scalar.activation(out=res[:], in_=products[(g, i)], func=ACT.Copy, scale=inv_deg[g][:, i : i + 1])
+            nc.sync.dma_start(out=out[t * E_TILE : (t + 1) * E_TILE, :], in_=res[:])
+
+        first_half = range(HALF)
+        second_half = range(HALF, GROUP)
 
         regroup_x()
-        filler(7)
-        degree_sums(*chunks[0])
-        for k, (g, c) in enumerate(chunks):
-            width = GROUP_TILES[g] * E_TILE
-            split = width * VECTOR_SHARE[k] // 16
-            last = k == len(chunks) - 1
-            grouped[(g, c)] = keep.tile([P, width, PACK], BF16, name="grouped_%d_%d" % (g, c), align_bytes=64)
-            codes[(g, c)] = keep.tile([P, width], U32, name="codes_%d_%d" % (g, c), align_bytes=64)
-            scales[(g, c)] = keep.tile([P, width], U8, name="scales_%d_%d" % (g, c), align_bytes=64)
+        quantize_x()
+        filler(10)
 
-            if not last:
-                if k < 2:
-                    filler(1)
-                if k + 1 < len(chunks) - 1:
-                    degree_sums(*chunks[k + 1])
-            else:
-                start_chain(g)
-                short_steps()
-            regroup(nc.vector.tensor_copy, grouped[(g, c)][:, :split, :], raw[(g, c)][:, :, :split])
-            short_steps()
-            regroup(nc.scalar.copy, grouped[(g, c)][:, split:, :], raw[(g, c)][:, :, split:])
-            for t in [t for t in multiplied if t in scaled and k >= len(chunks) - 2]:
-                multiplied.remove(t)
-                scale_and_store(t, on_vector=False)
-            if k == 0:
-                quantize_x()
-            elif k - 1 not in WHOLE:
-                quantize(*chunks[k - 1], 1)
-                short_steps()
-            if k == len(chunks) - 3:
-                quantize(g, c, 0)
-                degree_sums(*chunks[-1])
-                multiply()
-                start_chain(g)
-                short_steps()
-            elif k == len(chunks) - 2:
-                quantize(g, c, 0, SHARERS)
-                multiply()
-                short_steps()
-            elif not last:
-                quantize(g, c, 0)
-                multiply()
-                if c == LAST:
-                    start_chain(g)
-                short_steps()
-                if k in WHOLE:
-                    quantize(g, c, 1)
-                    multiply()
-                    short_steps()
-        for half in reversed(range(SHARERS)):
-            quantize(*chunks[-1], half)
-            multiply()
-            short_steps()
-        for t in multiplied:
-            scale_and_store(t, on_vector=True)
+        degree_sums(0, 0)
+        filler(2)
+        regroup_h(0, 0)
+        quantize(0, 0, first_half)
+        for i in first_half:
+            multiply(0, 0, i)
+
+        degree_sums(0, 1)
+        filler(2)
+        regroup_h(0, 1)
+        quantize(0, 0, second_half)
+        quantize(0, 1, first_half)
+        for i in first_half:
+            multiply(0, 1, i)
+
+        degree_sums(1, 0)
+        filler(1)
+        degree_sums(1, 1)
+        regroup_h(1, 0)
+        sum_passes(0)
+        quantize(0, 1, second_half)
+        for i in second_half:
+            multiply(0, 0, i)
+            multiply(0, 1, i)
+        make_safe(0)
+        quantize(1, 0, first_half)
+        for i in first_half:
+            multiply(1, 0, i)
+        invert(0)
+
+        regroup_h(1, 1)
+        mask(0)
+        for i in range(GROUP):
+            scale_and_store(0, i, on_vector=False)
+        sum_passes(1)
+        quantize(1, 0, second_half)
+        for i in second_half:
+            multiply(1, 0, i)
+        make_safe(1)
+        quantize(1, 1, first_half)
+        for i in first_half:
+            multiply(1, 1, i)
+        invert(1)
+        quantize(1, 1, second_half[:1])
+        multiply(1, 1, second_half[0])
+        mask(1)
+        quantize(1, 1, second_half[1:])
+        multiply(1, 1, second_half[1])
+        for i in range(GROUP):
+            scale_and_store(1, i, on_vector=(i % 2 == 1))

from contextlib import ExitStack

import concourse.mybir as mybir

BF16 = mybir.dt.bfloat16
F32 = mybir.dt.float32
U32 = mybir.dt.uint32
U8 = mybir.dt.uint8
FP8X4 = mybir.dt.float8_e4m3fn_x4
ALU = mybir.AluOpType
ACT = mybir.ActivationFunctionType
AXIS = mybir.AxisListType

P = 128
PACK = 4
K_PASS = P * PACK
VERTICES = 1024
EDGES = 1024
FEATURES = 128
PASSES = VERTICES // K_PASS
LAST = PASSES - 1
E_TILE = 128
RUN = 4
GROUP = 4
GROUPS = EDGES // E_TILE // GROUP
CHUNKS = [(g, c) for g in range(GROUPS) for c in range(PASSES)]
VECTOR_SHARE = (8, 8, 8, 9)
HALF = GROUP // 2
FILL = 256

FLOPS = 2 * VERTICES * EDGES * FEATURES


def regroup(copy, grouped, rows):
    copy(
        out=grouped.rearrange("p (g i) j -> p g j i", i=RUN),
        in_=rows.rearrange("p j (g i) -> p g j i", i=RUN),
    )


def tile_v2emsgpass_s_kernel(tc, X, H, out):
    nc = tc.nc
    with ExitStack() as ctx:
        keep = ctx.enter_context(tc.tile_pool(name="keep", bufs=1))
        psum = ctx.enter_context(tc.psum_pool(name="psum", bufs=1))
        ctx.enter_context(tc.manual_schedule())

        raw = {}
        x_raw = keep.tile([P, PASSES, PACK, FEATURES], BF16, name="x_raw")

        def load_x():
            nc.sync.dma_start(out=x_raw[:], in_=X.rearrange("(c p j) d -> p c j d", c=PASSES, j=PACK))

        def load(g, c):
            raw[(g, c)] = keep.tile([P, PACK, GROUP * E_TILE], BF16, name="raw_%d_%d" % (g, c))
            nc.sync.dma_start(
                out=raw[(g, c)][:],
                in_=H[
                    c * K_PASS : (c + 1) * K_PASS, g * GROUP * E_TILE : (g + 1) * GROUP * E_TILE
                ].rearrange("(p j) e -> p j e", j=PACK),
            )

        load_x()
        for g, c in CHUNKS:
            load(g, c)

        ones = keep.tile([P, 1], BF16, name="ones")
        nc.vector.memset(ones[:], 1.0)
        table_warm = keep.tile([P, 1], F32, name="table_warm")
        nc.scalar.activation(out=table_warm[:], in_=ones[:], func=ACT.Copy)
        fill = keep.tile([P, FILL * PACK], BF16, name="fill", align_bytes=64)
        fill_codes = keep.tile([P, FILL], U32, name="fill_codes", align_bytes=64)
        fill_scales = keep.tile([P, FILL], U8, name="fill_scales", align_bytes=64)
        nc.gpsimd.memset(fill[:], 1.0)
        nc.vector.quantize_mx(out=fill_codes[:].bitcast(FP8X4), scales=fill_scales[:], in_=fill[:])

        x_grouped = keep.tile([P, PASSES, FEATURES, PACK], BF16, name="x_grouped", align_bytes=64)
        x_codes = keep.tile([P, PASSES, FEATURES], U32, name="x_codes", align_bytes=64)
        x_scales = keep.tile([P, PASSES, FEATURES], U8, name="x_scales", align_bytes=64)
        grouped = {}
        codes = {}
        scales = {}
        for g, c in CHUNKS:
            width = GROUP * E_TILE
            grouped[(g, c)] = keep.tile([P, width, PACK], BF16, name="grouped_%d_%d" % (g, c), align_bytes=64)
            codes[(g, c)] = keep.tile([P, width], U32, name="codes_%d_%d" % (g, c), align_bytes=64)
            scales[(g, c)] = keep.tile([P, width], U8, name="scales_%d_%d" % (g, c), align_bytes=64)

        deg_sums = {}
        for g in range(GROUPS):
            deg_sums[g] = psum.tile([P, PASSES, GROUP], F32, name="deg_sums_%d" % g)
        products = {}
        for i in range(HALF):
            shared = psum.tile([P, 2 * FEATURES], F32, name="shared_%d" % i)
            products[(0, i)] = shared[:, :FEATURES]
            products[(0, HALF + i)] = shared[:, FEATURES:]
        bank = {}
        for i in range(GROUP):
            bank[i] = psum.tile([P, 2 * FEATURES], F32, name="bank_%d" % i)
            products[(1, i)] = bank[i][:, :FEATURES]
        deg = {}
        safe_deg = {}
        recip = {}
        inv_deg = {}
        for g in range(GROUPS):
            deg[g] = keep.tile([P, GROUP], F32, name="deg_%d" % g)
            safe_deg[g] = keep.tile([P, GROUP], F32, name="safe_deg_%d" % g)
            recip[g] = keep.tile([P, GROUP], F32, name="recip_%d" % g)
            inv_deg[g] = keep.tile([P, GROUP], F32, name="inv_deg_%d" % g)

        def filler(passes):
            for n in range(passes):
                nc.tensor.matmul_mx(
                    out=bank[GROUP - 1][:, :FILL],
                    lhsT=fill_codes[:, :E_TILE].bitcast(FP8X4),
                    lhsT_scale=fill_scales[:, :E_TILE],
                    rhs=fill_codes[:].bitcast(FP8X4),
                    rhs_scale=fill_scales[:],
                    start=True,
                    stop=True,
                )

        def degree_sums(g, c):
            for i in range(GROUP):
                for j in range(PACK):
                    nc.tensor.matmul(
                        out=deg_sums[g][:, c, i : i + 1],
                        lhsT=raw[(g, c)][:, j, i * E_TILE : (i + 1) * E_TILE],
                        rhs=ones[:],
                        start=(j == 0),
                        stop=(j == PACK - 1),
                    )

        def regroup_x():
            regroup(nc.vector.tensor_copy, x_grouped[:, 0], x_raw[:, 0])
            regroup(nc.scalar.copy, x_grouped[:, 1], x_raw[:, 1])

        def quantize_x():
            nc.vector.quantize_mx(
                out=x_codes[:].rearrange("p c d -> p (c d)").bitcast(FP8X4),
                scales=x_scales[:].rearrange("p c d -> p (c d)"),
                in_=x_grouped[:].rearrange("p c d j -> p (c d j)"),
            )

        def regroup_h(g, c):
            split = GROUP * E_TILE * VECTOR_SHARE[CHUNKS.index((g, c))] // 16
            regroup(nc.vector.tensor_copy, grouped[(g, c)][:, :split, :], raw[(g, c)][:, :, :split])
            regroup(nc.scalar.copy, grouped[(g, c)][:, split:, :], raw[(g, c)][:, :, split:])

        def quantize(g, c, tiles):
            cols = slice(tiles[0] * E_TILE, (tiles[-1] + 1) * E_TILE)
            nc.vector.quantize_mx(
                out=codes[(g, c)][:, cols].bitcast(FP8X4),
                scales=scales[(g, c)][:, cols],
                in_=grouped[(g, c)][:, cols, :].rearrange("p w j -> p (w j)"),
            )

        def multiply(g, c, i):
            nc.tensor.matmul_mx(
                out=products[(g, i)],
                lhsT=codes[(g, c)][:, i * E_TILE : (i + 1) * E_TILE].bitcast(FP8X4),
                lhsT_scale=scales[(g, c)][:, i * E_TILE : (i + 1) * E_TILE],
                rhs=x_codes[:, c, :].bitcast(FP8X4),
                rhs_scale=x_scales[:, c, :],
                start=(c == 0),
                stop=(c == LAST),
            )

        def sum_passes(g):
            nc.vector.tensor_reduce(
                out=deg[g][:], in_=deg_sums[g][:].rearrange("p c t -> p t c"), axis=AXIS.X, op=ALU.add
            )

        def make_safe(g):
            nc.vector.scalar_tensor_tensor(
                out=safe_deg[g][:], in0=deg[g][:], scalar=0.0, in1=deg[g][:], op0=ALU.is_equal, op1=ALU.add
            )

        def invert(g):
            nc.vector.reciprocal(out=recip[g][:], in_=safe_deg[g][:])

        def mask(g):
            nc.vector.scalar_tensor_tensor(
                out=inv_deg[g][:], in0=deg[g][:], scalar=0.0, in1=recip[g][:], op0=ALU.not_equal, op1=ALU.mult
            )

        def scale_and_store(g, i, on_vector):
            t = g * GROUP + i
            res = keep.tile([P, FEATURES], F32, name="res_%d" % t)
            if on_vector:
                nc.vector.tensor_scalar(
                    out=res[:], in0=products[(g, i)], scalar1=inv_deg[g][:, i : i + 1], scalar2=None, op0=ALU.mult
                )
            else:
                nc.scalar.activation(out=res[:], in_=products[(g, i)], func=ACT.Copy, scale=inv_deg[g][:, i : i + 1])
            nc.sync.dma_start(out=out[t * E_TILE : (t + 1) * E_TILE, :], in_=res[:])

        first_half = range(HALF)
        second_half = range(HALF, GROUP)

        regroup_x()
        quantize_x()
        filler(10)

        degree_sums(0, 0)
        filler(2)
        regroup_h(0, 0)
        quantize(0, 0, first_half)
        for i in first_half:
            multiply(0, 0, i)

        degree_sums(0, 1)
        filler(2)
        regroup_h(0, 1)
        quantize(0, 0, second_half)
        quantize(0, 1, first_half)
        for i in first_half:
            multiply(0, 1, i)

        degree_sums(1, 0)
        filler(1)
        degree_sums(1, 1)
        regroup_h(1, 0)
        sum_passes(0)
        quantize(0, 1, second_half)
        for i in second_half:
            multiply(0, 0, i)
            multiply(0, 1, i)
        make_safe(0)
        quantize(1, 0, first_half)
        for i in first_half:
            multiply(1, 0, i)
        invert(0)

        regroup_h(1, 1)
        mask(0)
        for i in range(GROUP):
            scale_and_store(0, i, on_vector=False)
        sum_passes(1)
        quantize(1, 0, second_half)
        for i in second_half:
            multiply(1, 0, i)
        make_safe(1)
        quantize(1, 1, first_half)
        for i in first_half:
            multiply(1, 1, i)
        invert(1)
        quantize(1, 1, second_half[:1])
        multiply(1, 1, second_half[0])
        mask(1)
        quantize(1, 1, second_half[1:])
        multiply(1, 1, second_half[1])
        for i in range(GROUP):
            scale_and_store(1, i, on_vector=(i % 2 == 1))
